import numpy as np
import ml_dtypes


def mxq(x, axis, fmt="e4m3"):
    dtype, down = {"e4m3": (ml_dtypes.float8_e4m3fn, 7), "e5m2": (ml_dtypes.float8_e5m2, 14)}[fmt]
    v = np.moveaxis(np.asarray(x, np.float32).astype(ml_dtypes.bfloat16).astype(np.float64), axis, -1)
    blocks = v.reshape(v.shape[:-1] + (-1, 32))
    amax = np.abs(blocks).max(-1, keepdims=True)
    byte = np.maximum(np.where(amax > 0, np.frexp(amax)[1] - 1 + 127, 0) - down, 1)
    scale = np.exp2(byte - 127.0)
    codes = (blocks / scale).astype(np.float32).astype(dtype).astype(np.float64)
    return np.moveaxis((codes * scale).reshape(v.shape), -1, axis)


WIDE = False


def mx_kscale(k):
    if not WIDE:
        return np.ones(k)
    levels = np.array([10, -10, 5, -5, 0])
    a = np.random.permutation(np.resize(levels, k // 512 * 4)).reshape(k // 512, 4)
    idx = np.arange(k)
    return np.exp2(a[idx // 512, idx % 128 // 32])


BF16 = ml_dtypes.bfloat16


def bf(x):
    return np.asarray(x, np.float32).astype(BF16)


def f64(x):
    return np.asarray(x).astype(np.float64)


N, M, D, F = 1024, 1024, 1024, 1024


def setup_inputs():
    s, t = mx_kscale(N), mx_kscale(D)
    return {"adj": bf((np.random.standard_normal((M, N)) / np.sqrt(D) + np.eye(M, N)) * s),
            "x": bf(np.random.standard_normal((N, D)) / s[:, None] * t),
            "weight": bf(np.random.standard_normal((D, F)) * np.sqrt(2.0 / D) / t[:, None])}


def reference(adj, x, weight):
    ax = mxq(f64(adj), 1, "e4m3") @ mxq(f64(x), 0, "e4m3")
    return mxq(ax, 1, "e4m3") @ mxq(f64(weight), 0, "e4m3")

@@ -1,0 +1,210 @@
+from contextlib import ExitStack
+
+import concourse.mybir as mybir
+from concourse.masks import make_identity
+
+FLOPS = 2 * 2 * 1024 * 1024 * 1024
+
+BF16 = mybir.dt.bfloat16
+F32 = mybir.dt.float32
+U32 = mybir.dt.uint32
+U8 = mybir.dt.uint8
+FP8X4 = mybir.dt.float8_e4m3fn_x4
+
+P = 128
+NB = 8
+HALF = 512
+
+ADJ_CHUNKS = ((0, 1), (1, 1), (2, 2), (4, 2), (6, 2))
+X_SCALAR_COLS = (160, 0)
+AX_ENGINES = ("SSVSSVSS", "SSSSSSSS")
+OUT_ENGINES = ("SSSVSSSV", "VSVSVSVS")
+
+
+def tile_graphconvolution_pb_kernel(tc, adj, x, weight, out):
+    nc = tc.nc
+    with ExitStack() as ctx:
+        keep = ctx.enter_context(tc.tile_pool(name="keep", bufs=1))
+        psum = ctx.enter_context(tc.psum_pool(name="psum", bufs=1))
+
+        def copy(letter, dst, src):
+            if letter == "V":
+                nc.vector.tensor_copy(out=dst, in_=src)
+            else:
+                nc.scalar.copy(out=dst, in_=src)
+
+        def quantise(codes, scales, grouped):
+            nc.vector.quantize_mx(out=codes.bitcast(FP8X4), scales=scales, in_=grouped)
+
+        def regroup(letter, dst, src):
+            copy(
+                letter,
+                dst.rearrange("p (c i t) -> p c t i", i=4, t=4),
+                src.rearrange("p t (c i) -> p c t i", i=4),
+            )
+
+        ident = keep.tile([P, P], F32, name="ident")
+        make_identity(nc, ident[:])
+
+        adj_v = adj.rearrange("(p b) j -> p b j", b=NB)
+        x_v = x.rearrange("(c u p e) d -> c u p e d", c=2, u=2, e=2)
+        w_v = weight.rearrange("(g t p) f -> g p t f", g=2, t=4)
+        out_v = out.rearrange("(p b) f -> p b f", b=NB)
+
+        araw, agrp, acod, asca = [], [], [], []
+        for k, (b0, nb) in enumerate(ADJ_CHUNKS):
+            araw.append(keep.tile([P, nb * 1024], BF16, name="araw%d" % k))
+            agrp.append(keep.tile([P, nb * 1024], BF16, name="agrp%d" % k, align_bytes=64))
+            acod.append(keep.tile([P, nb * 256], U32, name="acod%d" % k, align_bytes=64))
+            asca.append(keep.tile([P, nb * 256], U8, name="asca%d" % k, align_bytes=64))
+        xraw, xgrp, xcod, xsca = {}, {}, {}, {}
+        wgrp, wcod, wsca = {}, {}, {}
+        for h in range(2):
+            for c in range(2):
+                xraw[h, c] = keep.tile([P, 4, HALF], BF16, name="xraw%d%d" % (h, c))
+                xgrp[h, c] = keep.tile([P, 4 * HALF], BF16, name="xgrp%d%d" % (h, c), align_bytes=64)
+                xcod[h, c] = keep.tile([P, HALF], U32, name="xcod%d%d" % (h, c), align_bytes=64)
+                xsca[h, c] = keep.tile([P, HALF], U8, name="xsca%d%d" % (h, c), align_bytes=64)
+                wgrp[h, c] = keep.tile([P, 4 * HALF], BF16, name="wgrp%d%d" % (h, c), align_bytes=64)
+                wcod[h, c] = keep.tile([P, HALF], U32, name="wcod%d%d" % (h, c), align_bytes=64)
+                wsca[h, c] = keep.tile([P, HALF], U8, name="wsca%d%d" % (h, c), align_bytes=64)
+        wraw = [keep.tile([P, 4, 1024], BF16, name="wraw%d" % g) for g in range(2)]
+        axgrp, axcod, axsca = {}, {}, {}
+        for h in range(2):
+            for q in range(NB // 2):
+                axgrp[h, q] = keep.tile([P, 2 * HALF], BF16, name="axgrp%d%d" % (h, q), align_bytes=64)
+                axcod[h, q] = keep.tile([P, 2 * P], U32, name="axcod%d%d" % (h, q), align_bytes=64)
+                axsca[h, q] = keep.tile([P, 2 * P], U8, name="axsca%d%d" % (h, q), align_bytes=64)
+
+        def load_adj(k):
+            b0, nb = ADJ_CHUNKS[k]
+            nc.sync.dma_start(
+                out=araw[k][:].rearrange("p (b j) -> p b j", b=nb), in_=adj_v[:, b0 : b0 + nb, :]
+            )
+
+        def load_x(h):
+            for c in range(2):
+                for u in range(2):
+                    nc.sync.dma_start(
+                        out=xraw[h, c][:, 2 * u : 2 * u + 2, :],
+                        in_=x_v[c, u][:, :, HALF * h : HALF * (h + 1)],
+                    )
+
+        load_adj(0)
+        load_x(0)
+        for k in range(1, len(ADJ_CHUNKS)):
+            load_adj(k)
+        load_x(1)
+        for g in range(2):
+            nc.sync.dma_start(out=wraw[g][:], in_=w_v[g])
+
+        def adj_prep(k):
+            b0, nb = ADJ_CHUNKS[k]
+            words = araw[k][:].bitcast(F32)
+            gwords = agrp[k][:].bitcast(F32)
+            for bl in range(nb):
+                tp = psum.tile([P, 4, P], F32, name="tp", tag="tp", bufs=2)
+                for wb in range(4):
+                    lo = HALF * bl + P * wb
+                    nc.tensor.transpose(tp[:, wb, :], words[:, lo : lo + P], ident[:])
+                copy(
+                    "S",
+                    gwords[:, HALF * bl : HALF * (bl + 1)].rearrange("p (g i u) -> p g i u", g=2, u=2),
+                    tp[:].rearrange("p (g u) i -> p g i u", u=2),
+                )
+            quantise(acod[k][:], asca[k][:], agrp[k][:])
+
+        def x_prep(h):
+            ns = X_SCALAR_COLS[h]
+            for c in range(2):
+                nv = HALF - ns
+                regroup("V", xgrp[h, c][:, : 4 * nv], xraw[h, c][:, :, :nv])
+                if ns:
+                    regroup("S", xgrp[h, c][:, 4 * nv :], xraw[h, c][:, :, nv:])
+            for c in range(2):
+                quantise(xcod[h, c][:], xsca[h, c][:], xgrp[h, c][:])
+
+        def w_prep(fh):
+            for g in range(2):
+                regroup("V", wgrp[g, fh][:], wraw[g][:, :, HALF * fh : HALF * (fh + 1)])
+            for g in range(2):
+                quantise(wcod[g, fh][:], wsca[g, fh][:], wgrp[g, fh][:])
+
+        block_chunk = {}
+        for k, (b0, nb) in enumerate(ADJ_CHUNKS):
+            for bl in range(nb):
+                block_chunk[b0 + bl] = (k, bl)
+
+        def s1(h, b):
+            k, bl = block_chunk[b]
+            acc = psum.tile([P, 4, P], F32, name="acc1", tag="acc", bufs=6)
+            for t in range(4):
+                for c in range(2):
+                    lo = 2 * P * bl + P * c
+                    nc.tensor.matmul_mx(
+                        out=acc[:, t, :],
+                        lhsT=xcod[h, c][:, P * t : P * (t + 1)].bitcast(FP8X4),
+                        lhsT_scale=xsca[h, c][:, P * t : P * (t + 1)],
+                        rhs=acod[k][:, lo : lo + P].bitcast(FP8X4),
+                        rhs_scale=asca[k][:, lo : lo + P],
+                        start=(c == 0),
+                        stop=(c == 1),
+                    )
+            r = b % 2
+            copy(
+                AX_ENGINES[h][b],
+                axgrp[h, b // 2][:, HALF * r : HALF * (r + 1)].rearrange("p (i t) -> p i t", t=4),
+                acc[:].rearrange("p t i -> p i t"),
+            )
+
+        def ax_q(h, q):
+            quantise(axcod[h, q][:], axsca[h, q][:], axgrp[h, q][:])
+
+        def s2(fh, b):
+            acc = psum.tile([P, HALF], F32, name="acc2", tag="acc", bufs=6)
+            r = b % 2
+            for h in range(2):
+                nc.tensor.matmul_mx(
+                    out=acc[:],
+                    lhsT=axcod[h, b // 2][:, P * r : P * (r + 1)].bitcast(FP8X4),
+                    lhsT_scale=axsca[h, b // 2][:, P * r : P * (r + 1)],
+                    rhs=wcod[h, fh][:].bitcast(FP8X4),
+                    rhs_scale=wsca[h, fh][:],
+                    start=(h == 0),
+                    stop=(h == 1),
+                )
+            res = keep.tile([P, HALF], F32, name="res%d%d" % (fh, b))
+            copy(OUT_ENGINES[fh][b], res[:], acc[:])
+            nc.sync.dma_start(out=out_v[:, b, HALF * fh : HALF * (fh + 1)], in_=res[:])
+
+        adj_prep(0)
+        x_prep(0)
+        adj_prep(1)
+        adj_prep(2)
+        s1(0, 0)
+        s1(0, 1)
+        adj_prep(3)
+        s1(0, 2)
+        s1(0, 3)
+        adj_prep(4)
+        x_prep(1)
+        ax_q(0, 0)
+        s1(0, 4)
+        s1(0, 5)
+        ax_q(0, 1)
+        s1(0, 6)
+        s1(0, 7)
+        ax_q(0, 2)
+        ax_q(0, 3)
+        for b in range(NB):
+            s1(1, b)
+            if b == 3:
+                w_prep(0)
+            if b % 2 == 1:
+                ax_q(1, b // 2)
+        for b in range(NB):
+            s2(0, b)
+            if b == 1:
+                w_prep(1)
+        for b in range(NB):
+            s2(1, b)

@@ -14,31 +14,20 @@ FP8X4 = mybir.dt.float8_e4m3fn_x4
 P = 128
 NB = 8
 HALF = 512
-
-ADJ_CHUNKS = ((0, 1), (1, 1), (2, 2), (4, 2), (6, 2))
-X_SCALAR_COLS = (160, 0)
-AX_ENGINES = ("SSVSSVSS", "SSSSSSSS")
-OUT_ENGINES = ("SSSVSSSV", "VSVSVSVS")
+X_SCALAR_COLS = 160
 
 
 def tile_graphconvolution_pb_kernel(tc, adj, x, weight, out):
     nc = tc.nc
     with ExitStack() as ctx:
         keep = ctx.enter_context(tc.tile_pool(name="keep", bufs=1))
-        psum = ctx.enter_context(tc.psum_pool(name="psum", bufs=1))
-
-        def copy(letter, dst, src):
-            if letter == "V":
-                nc.vector.tensor_copy(out=dst, in_=src)
-            else:
-                nc.scalar.copy(out=dst, in_=src)
+        psum = ctx.enter_context(tc.psum_pool(name="psum", bufs=8))
 
         def quantise(codes, scales, grouped):
             nc.vector.quantize_mx(out=codes.bitcast(FP8X4), scales=scales, in_=grouped)
 
-        def regroup(letter, dst, src):
-            copy(
-                letter,
+        def regroup_views(dst, src):
+            return (
                 dst.rearrange("p (c i t) -> p c t i", i=4, t=4),
                 src.rearrange("p t (c i) -> p c t i", i=4),
             )
@@ -52,13 +41,14 @@ def tile_graphconvolution_pb_kernel(tc, adj, x, weight, out):
         out_v = out.rearrange("(p b) f -> p b f", b=NB)
 
         araw, agrp, acod, asca = [], [], [], []
-        for k, (b0, nb) in enumerate(ADJ_CHUNKS):
-            araw.append(keep.tile([P, nb * 1024], BF16, name="araw%d" % k))
-            agrp.append(keep.tile([P, nb * 1024], BF16, name="agrp%d" % k, align_bytes=64))
-            acod.append(keep.tile([P, nb * 256], U32, name="acod%d" % k, align_bytes=64))
-            asca.append(keep.tile([P, nb * 256], U8, name="asca%d" % k, align_bytes=64))
+        for q in range(NB // 2):
+            araw.append(keep.tile([P, 2 * 1024], BF16, name="araw%d" % q))
+            agrp.append(keep.tile([P, 2 * 1024], BF16, name="agrp%d" % q, align_bytes=64))
+            acod.append(keep.tile([P, 2 * 256], U32, name="acod%d" % q, align_bytes=64))
+            asca.append(keep.tile([P, 2 * 256], U8, name="asca%d" % q, align_bytes=64))
         xraw, xgrp, xcod, xsca = {}, {}, {}, {}
         wgrp, wcod, wsca = {}, {}, {}
+        axgrp, axcod, axsca = {}, {}, {}
         for h in range(2):
             for c in range(2):
                 xraw[h, c] = keep.tile([P, 4, HALF], BF16, name="xraw%d%d" % (h, c))
@@ -68,18 +58,15 @@ def tile_graphconvolution_pb_kernel(tc, adj, x, weight, out):
                 wgrp[h, c] = keep.tile([P, 4 * HALF], BF16, name="wgrp%d%d" % (h, c), align_bytes=64)
                 wcod[h, c] = keep.tile([P, HALF], U32, name="wcod%d%d" % (h, c), align_bytes=64)
                 wsca[h, c] = keep.tile([P, HALF], U8, name="wsca%d%d" % (h, c), align_bytes=64)
-        wraw = [keep.tile([P, 4, 1024], BF16, name="wraw%d" % g) for g in range(2)]
-        axgrp, axcod, axsca = {}, {}, {}
-        for h in range(2):
             for q in range(NB // 2):
                 axgrp[h, q] = keep.tile([P, 2 * HALF], BF16, name="axgrp%d%d" % (h, q), align_bytes=64)
                 axcod[h, q] = keep.tile([P, 2 * P], U32, name="axcod%d%d" % (h, q), align_bytes=64)
                 axsca[h, q] = keep.tile([P, 2 * P], U8, name="axsca%d%d" % (h, q), align_bytes=64)
+        wraw = [keep.tile([P, 4, 1024], BF16, name="wraw%d" % g) for g in range(2)]
 
-        def load_adj(k):
-            b0, nb = ADJ_CHUNKS[k]
+        def load_adj(q):
             nc.sync.dma_start(
-                out=araw[k][:].rearrange("p (b j) -> p b j", b=nb), in_=adj_v[:, b0 : b0 + nb, :]
+                out=araw[q][:].rearrange("p (b j) -> p b j", b=2), in_=adj_v[:, 2 * q : 2 * q + 2, :]
             )
 
         def load_x(h):
@@ -90,121 +77,128 @@ def tile_graphconvolution_pb_kernel(tc, adj, x, weight, out):
                         in_=x_v[c, u][:, :, HALF * h : HALF * (h + 1)],
                     )
 
-        load_adj(0)
-        load_x(0)
-        for k in range(1, len(ADJ_CHUNKS)):
-            load_adj(k)
-        load_x(1)
-        for g in range(2):
-            nc.sync.dma_start(out=wraw[g][:], in_=w_v[g])
-
-        def adj_prep(k):
-            b0, nb = ADJ_CHUNKS[k]
-            words = araw[k][:].bitcast(F32)
-            gwords = agrp[k][:].bitcast(F32)
-            for bl in range(nb):
-                tp = psum.tile([P, 4, P], F32, name="tp", tag="tp", bufs=2)
+        def transpose_adj(q):
+            words = araw[q][:].bitcast(F32)
+            gwords = agrp[q][:].bitcast(F32)
+            for r in range(2):
+                tp = psum.tile([P, 4, P], F32, name="tp", tag="bank")
                 for wb in range(4):
-                    lo = HALF * bl + P * wb
+                    lo = HALF * r + P * wb
                     nc.tensor.transpose(tp[:, wb, :], words[:, lo : lo + P], ident[:])
-                copy(
-                    "S",
-                    gwords[:, HALF * bl : HALF * (bl + 1)].rearrange("p (g i u) -> p g i u", g=2, u=2),
-                    tp[:].rearrange("p (g u) i -> p g i u", u=2),
+                nc.scalar.copy(
+                    out=gwords[:, HALF * r : HALF * (r + 1)].rearrange("p (g i u) -> p g i u", g=2, u=2),
+                    in_=tp[:].rearrange("p (g u) i -> p g i u", u=2),
                 )
-            quantise(acod[k][:], asca[k][:], agrp[k][:])
 
-        def x_prep(h):
-            ns = X_SCALAR_COLS[h]
-            for c in range(2):
-                nv = HALF - ns
-                regroup("V", xgrp[h, c][:, : 4 * nv], xraw[h, c][:, :, :nv])
-                if ns:
-                    regroup("S", xgrp[h, c][:, 4 * nv :], xraw[h, c][:, :, nv:])
-            for c in range(2):
-                quantise(xcod[h, c][:], xsca[h, c][:], xgrp[h, c][:])
+        def quantise_adj(q):
+            quantise(acod[q][:], asca[q][:], agrp[q][:])
 
-        def w_prep(fh):
-            for g in range(2):
-                regroup("V", wgrp[g, fh][:], wraw[g][:, :, HALF * fh : HALF * (fh + 1)])
-            for g in range(2):
-                quantise(wcod[g, fh][:], wsca[g, fh][:], wgrp[g, fh][:])
+        def regroup_x(h, c, scalar_cols):
+            nv = HALF - scalar_cols
+            dst, src = regroup_views(xgrp[h, c][:, : 4 * nv], xraw[h, c][:, :, :nv])
+            nc.vector.tensor_copy(out=dst, in_=src)
+            if scalar_cols:
+                dst, src = regroup_views(xgrp[h, c][:, 4 * nv :], xraw[h, c][:, :, nv:])
+                nc.scalar.copy(out=dst, in_=src)
 
-        block_chunk = {}
-        for k, (b0, nb) in enumerate(ADJ_CHUNKS):
-            for bl in range(nb):
-                block_chunk[b0 + bl] = (k, bl)
+        def quantise_x(h, c):
+            quantise(xcod[h, c][:], xsca[h, c][:], xgrp[h, c][:])
 
-        def s1(h, b):
-            k, bl = block_chunk[b]
-            acc = psum.tile([P, 4, P], F32, name="acc1", tag="acc", bufs=6)
+        def regroup_w(fh, g):
+            dst, src = regroup_views(wgrp[g, fh][:], wraw[g][:, :, HALF * fh : HALF * (fh + 1)])
+            nc.vector.tensor_copy(out=dst, in_=src)
+
+        def quantise_w(fh, g):
+            quantise(wcod[g, fh][:], wsca[g, fh][:], wgrp[g, fh][:])
+
+        def stage1(h, b):
+            q, r = b // 2, b % 2
+            acc = psum.tile([P, 4, P], F32, name="acc1", tag="bank")
             for t in range(4):
                 for c in range(2):
-                    lo = 2 * P * bl + P * c
+                    lo = 2 * P * r + P * c
                     nc.tensor.matmul_mx(
                         out=acc[:, t, :],
                         lhsT=xcod[h, c][:, P * t : P * (t + 1)].bitcast(FP8X4),
                         lhsT_scale=xsca[h, c][:, P * t : P * (t + 1)],
-                        rhs=acod[k][:, lo : lo + P].bitcast(FP8X4),
-                        rhs_scale=asca[k][:, lo : lo + P],
+                        rhs=acod[q][:, lo : lo + P].bitcast(FP8X4),
+                        rhs_scale=asca[q][:, lo : lo + P],
                         start=(c == 0),
                         stop=(c == 1),
                     )
-            r = b % 2
-            copy(
-                AX_ENGINES[h][b],
-                axgrp[h, b // 2][:, HALF * r : HALF * (r + 1)].rearrange("p (i t) -> p i t", t=4),
-                acc[:].rearrange("p t i -> p i t"),
+            nc.scalar.copy(
+                out=axgrp[h, q][:, HALF * r : HALF * (r + 1)].rearrange("p (i t) -> p i t", t=4),
+                in_=acc[:].rearrange("p t i -> p i t"),
             )
 
-        def ax_q(h, q):
+        def quantise_ax(h, q):
             quantise(axcod[h, q][:], axsca[h, q][:], axgrp[h, q][:])
 
-        def s2(fh, b):
-            acc = psum.tile([P, HALF], F32, name="acc2", tag="acc", bufs=6)
-            r = b % 2
+        def stage2(fh, b, on_vector):
+            q, r = b // 2, b % 2
+            acc = psum.tile([P, HALF], F32, name="acc2", tag="bank")
             for h in range(2):
                 nc.tensor.matmul_mx(
                     out=acc[:],
-                    lhsT=axcod[h, b // 2][:, P * r : P * (r + 1)].bitcast(FP8X4),
-                    lhsT_scale=axsca[h, b // 2][:, P * r : P * (r + 1)],
+                    lhsT=axcod[h, q][:, P * r : P * (r + 1)].bitcast(FP8X4),
+                    lhsT_scale=axsca[h, q][:, P * r : P * (r + 1)],
                     rhs=wcod[h, fh][:].bitcast(FP8X4),
                     rhs_scale=wsca[h, fh][:],
                     start=(h == 0),
                     stop=(h == 1),
                 )
             res = keep.tile([P, HALF], F32, name="res%d%d" % (fh, b))
-            copy(OUT_ENGINES[fh][b], res[:], acc[:])
+            if on_vector:
+                nc.vector.tensor_copy(out=res[:], in_=acc[:])
+            else:
+                nc.scalar.copy(out=res[:], in_=acc[:])
             nc.sync.dma_start(out=out_v[:, b, HALF * fh : HALF * (fh + 1)], in_=res[:])
 
-        adj_prep(0)
-        x_prep(0)
-        adj_prep(1)
-        adj_prep(2)
-        s1(0, 0)
-        s1(0, 1)
-        adj_prep(3)
-        s1(0, 2)
-        s1(0, 3)
-        adj_prep(4)
-        x_prep(1)
-        ax_q(0, 0)
-        s1(0, 4)
-        s1(0, 5)
-        ax_q(0, 1)
-        s1(0, 6)
-        s1(0, 7)
-        ax_q(0, 2)
-        ax_q(0, 3)
-        for b in range(NB):
-            s1(1, b)
-            if b == 3:
-                w_prep(0)
-            if b % 2 == 1:
-                ax_q(1, b // 2)
-        for b in range(NB):
-            s2(0, b)
-            if b == 1:
-                w_prep(1)
-        for b in range(NB):
-            s2(1, b)
+        with tc.manual_schedule():
+            load_adj(0)
+            load_adj(1)
+            load_x(0)
+            load_adj(2)
+            load_adj(3)
+            load_x(1)
+            for g in range(2):
+                nc.sync.dma_start(out=wraw[g][:], in_=w_v[g])
+
+            transpose_adj(0)
+            transpose_adj(1)
+            quantise_adj(0)
+            regroup_x(0, 0, X_SCALAR_COLS)
+            quantise_adj(1)
+            quantise_x(0, 0)
+            regroup_x(0, 1, X_SCALAR_COLS)
+            transpose_adj(2)
+            transpose_adj(3)
+            quantise_x(0, 1)
+            quantise_adj(2)
+            regroup_x(1, 0, 0)
+            quantise_adj(3)
+            quantise_x(1, 0)
+            regroup_x(1, 1, 0)
+            quantise_x(1, 1)
+
+            for h in range(2):
+                for b in range(NB):
+                    stage1(h, b)
+
+            for g in range(2):
+                regroup_w(0, g)
+                quantise_ax(0, 2 * g)
+                quantise_ax(0, 2 * g + 1)
+                quantise_w(0, g)
+            quantise_ax(1, 0)
+            quantise_ax(1, 1)
+            for g in range(2):
+                regroup_w(1, g)
+                quantise_ax(1, 2 + g)
+            for g in range(2):
+                quantise_w(1, g)
+
+            for b in range(NB):
+                stage2(0, b, False)
+            for b in range(NB):
+                stage2(1, b, b % 2 == 0)

@@ -90,6 +90,14 @@ def tile_graphconvolution_pb_kernel(tc, adj, x, weight, out):
                     in_=tp[:].rearrange("p (g u) i -> p g i u", u=2),
                 )
 
+        warm = psum.tile([P, HALF], F32, name="warm", tag="bank")
+
+        def keep_clock_up(tile_2d, times):
+            for n in range(times):
+                nc.tensor.matmul(
+                    out=warm[:], lhsT=tile_2d[:, :P], rhs=tile_2d[:, :HALF], start=True, stop=True
+                )
+
         def quantise_adj(q):
             quantise(acod[q][:], asca[q][:], agrp[q][:])
 
@@ -171,7 +179,10 @@ def tile_graphconvolution_pb_kernel(tc, adj, x, weight, out):
             quantise_adj(1)
             quantise_x(0, 0)
             regroup_x(0, 1, X_SCALAR_COLS)
+            keep_clock_up(xraw[0, 0][:, 3, :], 3)
+            keep_clock_up(xraw[0, 1][:, 3, :], 3)
             transpose_adj(2)
+            keep_clock_up(araw[2][:], 2)
             transpose_adj(3)
             quantise_x(0, 1)
             quantise_adj(2)

@@ -14,6 +14,7 @@ FP8X4 = mybir.dt.float8_e4m3fn_x4
 P = 128
 NB = 8
 HALF = 512
+QUARTER = 256
 X_SCALAR_COLS = 160
 
 
@@ -32,6 +33,14 @@ def tile_graphconvolution_pb_kernel(tc, adj, x, weight, out):
                 src.rearrange("p t (c i) -> p c t i", i=4),
             )
 
+        def copy_on(engine, dst, src):
+            if engine is nc.vector:
+                nc.vector.tensor_copy(out=dst, in_=src)
+            else:
+                nc.scalar.copy(out=dst, in_=src)
+
+        zeros = keep.tile([P, HALF], BF16, name="zeros")
+        nc.vector.memset(zeros[:], 0.0)
         ident = keep.tile([P, P], F32, name="ident")
         make_identity(nc, ident[:])
 
@@ -64,69 +73,76 @@ def tile_graphconvolution_pb_kernel(tc, adj, x, weight, out):
                 axsca[h, q] = keep.tile([P, 2 * P], U8, name="axsca%d%d" % (h, q), align_bytes=64)
         wraw = [keep.tile([P, 4, 1024], BF16, name="wraw%d" % g) for g in range(2)]
 
-        def load_adj(q):
+        def load_adj(q, blocks=(0, 1)):
+            lo, n = blocks[0], len(blocks)
             nc.sync.dma_start(
-                out=araw[q][:].rearrange("p (b j) -> p b j", b=2), in_=adj_v[:, 2 * q : 2 * q + 2, :]
+                out=araw[q][:, 1024 * lo : 1024 * (lo + n)].rearrange("p (b j) -> p b j", b=n),
+                in_=adj_v[:, 2 * q + lo : 2 * q + lo + n, :],
             )
 
-        def load_x(h):
-            for c in range(2):
-                for u in range(2):
-                    nc.sync.dma_start(
-                        out=xraw[h, c][:, 2 * u : 2 * u + 2, :],
-                        in_=x_v[c, u][:, :, HALF * h : HALF * (h + 1)],
-                    )
+        def load_x(h, c, lo=0, hi=HALF):
+            for u in range(2):
+                nc.sync.dma_start(
+                    out=xraw[h, c][:, 2 * u : 2 * u + 2, lo:hi],
+                    in_=x_v[c, u][:, :, HALF * h + lo : HALF * h + hi],
+                )
 
-        def transpose_adj(q):
+        def load_w(g, lo=0, hi=1024):
+            nc.sync.dma_start(out=wraw[g][:, :, lo:hi], in_=w_v[g][:, :, lo:hi])
+
+        def transpose_adj(b, engine=None):
+            q, r = b // 2, b % 2
             words = araw[q][:].bitcast(F32)
             gwords = agrp[q][:].bitcast(F32)
-            for r in range(2):
-                tp = psum.tile([P, 4, P], F32, name="tp", tag="bank")
-                for wb in range(4):
-                    lo = HALF * r + P * wb
-                    nc.tensor.transpose(tp[:, wb, :], words[:, lo : lo + P], ident[:])
-                nc.scalar.copy(
-                    out=gwords[:, HALF * r : HALF * (r + 1)].rearrange("p (g i u) -> p g i u", g=2, u=2),
-                    in_=tp[:].rearrange("p (g u) i -> p g i u", u=2),
-                )
-
-        warm = psum.tile([P, HALF], F32, name="warm", tag="bank")
+            tp = psum.tile([P, 4, P], F32, name="tp", tag="bank")
+            for wb in range(4):
+                lo = HALF * r + P * wb
+                nc.tensor.transpose(tp[:, wb, :], words[:, lo : lo + P], ident[:])
+            copy_on(
+                engine or nc.scalar,
+                gwords[:, HALF * r : HALF * (r + 1)].rearrange("p (g i u) -> p g i u", g=2, u=2),
+                tp[:].rearrange("p (g u) i -> p g i u", u=2),
+            )
 
         def keep_clock_up(tile_2d, times):
-            for n in range(times):
-                nc.tensor.matmul(
-                    out=warm[:], lhsT=tile_2d[:, :P], rhs=tile_2d[:, :HALF], start=True, stop=True
-                )
+            n = min(HALF, tile_2d.shape[1])
+            warm = psum.tile([P, HALF], F32, name="warm", tag="bank")
+            for i in range(times):
+                nc.tensor.matmul(out=warm[:, :n], lhsT=tile_2d[:, :P], rhs=tile_2d[:, :n], start=True, stop=True)
 
-        def quantise_adj(q):
-            quantise(acod[q][:], asca[q][:], agrp[q][:])
+        def quantise_adj(q, blocks=(0, 1)):
+            lo, hi = blocks[0], blocks[-1] + 1
+            quantise(
+                acod[q][:, 256 * lo : 256 * hi], asca[q][:, 256 * lo : 256 * hi], agrp[q][:, 1024 * lo : 1024 * hi]
+            )
 
-        def regroup_x(h, c, scalar_cols):
-            nv = HALF - scalar_cols
-            dst, src = regroup_views(xgrp[h, c][:, : 4 * nv], xraw[h, c][:, :, :nv])
-            nc.vector.tensor_copy(out=dst, in_=src)
-            if scalar_cols:
-                dst, src = regroup_views(xgrp[h, c][:, 4 * nv :], xraw[h, c][:, :, nv:])
-                nc.scalar.copy(out=dst, in_=src)
+        def regroup_x(h, c, engine, lo=0, hi=HALF):
+            dst, src = regroup_views(xgrp[h, c][:, 4 * lo : 4 * hi], xraw[h, c][:, :, lo:hi])
+            copy_on(engine, dst, src)
 
-        def quantise_x(h, c):
-            quantise(xcod[h, c][:], xsca[h, c][:], xgrp[h, c][:])
+        def quantise_x(h, c, lo=0, hi=HALF):
+            quantise(xcod[h, c][:, lo:hi], xsca[h, c][:, lo:hi], xgrp[h, c][:, 4 * lo : 4 * hi])
 
-        def regroup_w(fh, g):
-            dst, src = regroup_views(wgrp[g, fh][:], wraw[g][:, :, HALF * fh : HALF * (fh + 1)])
-            nc.vector.tensor_copy(out=dst, in_=src)
+        def regroup_w(fh, g, engine, lo=0, hi=HALF):
+            dst, src = regroup_views(
+                wgrp[g, fh][:, 4 * lo : 4 * hi], wraw[g][:, :, HALF * fh + lo : HALF * fh + hi]
+            )
+            copy_on(engine, dst, src)
 
         def quantise_w(fh, g):
             quantise(wcod[g, fh][:], wsca[g, fh][:], wgrp[g, fh][:])
 
-        def stage1(h, b):
+        acc1 = {}
+
+        def stage1_passes(h, b, tiles):
             q, r = b // 2, b % 2
-            acc = psum.tile([P, 4, P], F32, name="acc1", tag="bank")
-            for t in range(4):
+            if (h, b) not in acc1:
+                acc1[h, b] = psum.tile([P, 4, P], F32, name="acc1", tag="bank")
+            for t in tiles:
                 for c in range(2):
                     lo = 2 * P * r + P * c
                     nc.tensor.matmul_mx(
-                        out=acc[:, t, :],
+                        out=acc1[h, b][:, t, :],
                         lhsT=xcod[h, c][:, P * t : P * (t + 1)].bitcast(FP8X4),
                         lhsT_scale=xsca[h, c][:, P * t : P * (t + 1)],
                         rhs=acod[q][:, lo : lo + P].bitcast(FP8X4),
@@ -134,82 +150,99 @@ def tile_graphconvolution_pb_kernel(tc, adj, x, weight, out):
                         start=(c == 0),
                         stop=(c == 1),
                     )
-            nc.scalar.copy(
-                out=axgrp[h, q][:, HALF * r : HALF * (r + 1)].rearrange("p (i t) -> p i t", t=4),
-                in_=acc[:].rearrange("p t i -> p i t"),
+
+        def stage1_out(h, b, engine):
+            q, r = b // 2, b % 2
+            copy_on(
+                engine,
+                axgrp[h, q][:, HALF * r : HALF * (r + 1)].rearrange("p (i t) -> p i t", t=4),
+                acc1[h, b][:].rearrange("p t i -> p i t"),
             )
+
+        def stage1(h, b, engine=None):
+            stage1_passes(h, b, range(4))
+            stage1_out(h, b, engine or nc.scalar)
 
         def quantise_ax(h, q):
             quantise(axcod[h, q][:], axsca[h, q][:], axgrp[h, q][:])
 
-        def stage2(fh, b, on_vector):
+        def stage2(fh, b, engines):
             q, r = b // 2, b % 2
-            acc = psum.tile([P, HALF], F32, name="acc2", tag="bank")
-            for h in range(2):
-                nc.tensor.matmul_mx(
-                    out=acc[:],
-                    lhsT=axcod[h, q][:, P * r : P * (r + 1)].bitcast(FP8X4),
-                    lhsT_scale=axsca[h, q][:, P * r : P * (r + 1)],
-                    rhs=wcod[h, fh][:].bitcast(FP8X4),
-                    rhs_scale=wsca[h, fh][:],
-                    start=(h == 0),
-                    stop=(h == 1),
-                )
-            res = keep.tile([P, HALF], F32, name="res%d%d" % (fh, b))
-            if on_vector:
-                nc.vector.tensor_copy(out=res[:], in_=acc[:])
-            else:
-                nc.scalar.copy(out=res[:], in_=acc[:])
-            nc.sync.dma_start(out=out_v[:, b, HALF * fh : HALF * (fh + 1)], in_=res[:])
+            n = HALF // len(engines)
+            for i, engine in enumerate(engines):
+                acc = psum.tile([P, n], F32, name="acc2", tag="bank")
+                for h in range(2):
+                    nc.tensor.matmul_mx(
+                        out=acc[:],
+                        lhsT=axcod[h, q][:, P * r : P * (r + 1)].bitcast(FP8X4),
+                        lhsT_scale=axsca[h, q][:, P * r : P * (r + 1)],
+                        rhs=wcod[h, fh][:, n * i : n * (i + 1)].bitcast(FP8X4),
+                        rhs_scale=wsca[h, fh][:, n * i : n * (i + 1)],
+                        start=(h == 0),
+                        stop=(h == 1),
+                    )
+                res = keep.tile([P, n], F32, name="res%d%d%d" % (fh, b, i))
+                copy_on(engine, res[:], acc[:])
+                lo = HALF * fh + n * i
+                nc.sync.dma_start(out=out_v[:, b, lo : lo + n], in_=res[:])
 
+        V, S = nc.vector, nc.scalar
         with tc.manual_schedule():
             load_adj(0)
             load_adj(1)
-            load_x(0)
+            load_x(0, 0)
+            load_x(0, 1)
             load_adj(2)
             load_adj(3)
-            load_x(1)
+            load_x(1, 0)
+            load_x(1, 1)
             for g in range(2):
-                nc.sync.dma_start(out=wraw[g][:], in_=w_v[g])
-
+                load_w(g)
+            keep_clock_up(zeros[:], 6)
             transpose_adj(0)
             transpose_adj(1)
+            keep_clock_up(zeros[:], 2)
+            transpose_adj(2)
+            transpose_adj(3)
+            keep_clock_up(zeros[:], 2)
             quantise_adj(0)
-            regroup_x(0, 0, X_SCALAR_COLS)
+            regroup_x(0, 0, V, 0, HALF - X_SCALAR_COLS)
+            regroup_x(0, 0, S, HALF - X_SCALAR_COLS, HALF)
             quantise_adj(1)
             quantise_x(0, 0)
-            regroup_x(0, 1, X_SCALAR_COLS)
-            keep_clock_up(xraw[0, 0][:, 3, :], 3)
-            keep_clock_up(xraw[0, 1][:, 3, :], 3)
-            transpose_adj(2)
-            keep_clock_up(araw[2][:], 2)
-            transpose_adj(3)
+            regroup_x(0, 1, V, 0, HALF - X_SCALAR_COLS)
+            regroup_x(0, 1, S, HALF - X_SCALAR_COLS, HALF)
+            keep_clock_up(xraw[0, 0][:, 3, :], 2)
+            keep_clock_up(xraw[0, 1][:, 3, :], 2)
+            transpose_adj(4)
+            transpose_adj(5)
+            transpose_adj(6)
+            transpose_adj(7)
             quantise_x(0, 1)
             quantise_adj(2)
-            regroup_x(1, 0, 0)
+            regroup_x(1, 0, V)
             quantise_adj(3)
             quantise_x(1, 0)
-            regroup_x(1, 1, 0)
+            regroup_x(1, 1, V)
             quantise_x(1, 1)
+            for b in range(NB):
+                stage1(0, b)
 
-            for h in range(2):
-                for b in range(NB):
-                    stage1(h, b)
-
+            for b in range(NB):
+                stage1(1, b)
             for g in range(2):
-                regroup_w(0, g)
+                regroup_w(0, g, V)
                 quantise_ax(0, 2 * g)
                 quantise_ax(0, 2 * g + 1)
                 quantise_w(0, g)
             quantise_ax(1, 0)
             quantise_ax(1, 1)
             for g in range(2):
-                regroup_w(1, g)
+                regroup_w(1, g, V)
                 quantise_ax(1, 2 + g)
             for g in range(2):
                 quantise_w(1, g)
-
             for b in range(NB):
-                stage2(0, b, False)
+                stage2(0, b, (S,))
             for b in range(NB):
-                stage2(1, b, b % 2 == 0)
+                stage2(1, b, (V if b % 2 == 0 else S,))

@@ -208,22 +208,24 @@ def tile_graphconvolution_pb_kernel(tc, adj, x, weight, out):
             quantise_adj(0)
             regroup_x(0, 0, V, 0, HALF - X_SCALAR_COLS)
             regroup_x(0, 0, S, HALF - X_SCALAR_COLS, HALF)
-            quantise_adj(1)
             quantise_x(0, 0)
             regroup_x(0, 1, V, 0, HALF - X_SCALAR_COLS)
             regroup_x(0, 1, S, HALF - X_SCALAR_COLS, HALF)
+            quantise_adj(1)
             keep_clock_up(xraw[0, 0][:, 3, :], 2)
-            keep_clock_up(xraw[0, 1][:, 3, :], 2)
+            keep_clock_up(xraw[0, 1][:, 3, :], 3)
             transpose_adj(4)
             transpose_adj(5)
+            keep_clock_up(zeros[:], 1)
             transpose_adj(6)
             transpose_adj(7)
+            keep_clock_up(zeros[:], 1)
             quantise_x(0, 1)
             quantise_adj(2)
             regroup_x(1, 0, V)
             quantise_adj(3)
-            quantise_x(1, 0)
             regroup_x(1, 1, V)
+            quantise_x(1, 0)
             quantise_x(1, 1)
             for b in range(NB):
                 stage1(0, b)

from contextlib import ExitStack

import concourse.mybir as mybir
from concourse.masks import make_identity

FLOPS = 2 * 2 * 1024 * 1024 * 1024

BF16 = mybir.dt.bfloat16
F32 = mybir.dt.float32
U32 = mybir.dt.uint32
U8 = mybir.dt.uint8
FP8X4 = mybir.dt.float8_e4m3fn_x4

P = 128
NB = 8
HALF = 512
QUARTER = 256
X_SCALAR_COLS = 160


def tile_graphconvolution_pb_kernel(tc, adj, x, weight, out):
    nc = tc.nc
    with ExitStack() as ctx:
        keep = ctx.enter_context(tc.tile_pool(name="keep", bufs=1))
        psum = ctx.enter_context(tc.psum_pool(name="psum", bufs=8))

        def quantise(codes, scales, grouped):
            nc.vector.quantize_mx(out=codes.bitcast(FP8X4), scales=scales, in_=grouped)

        def regroup_views(dst, src):
            return (
                dst.rearrange("p (c i t) -> p c t i", i=4, t=4),
                src.rearrange("p t (c i) -> p c t i", i=4),
            )

        def copy_on(engine, dst, src):
            if engine is nc.vector:
                nc.vector.tensor_copy(out=dst, in_=src)
            else:
                nc.scalar.copy(out=dst, in_=src)

        zeros = keep.tile([P, HALF], BF16, name="zeros")
        nc.vector.memset(zeros[:], 0.0)
        ident = keep.tile([P, P], F32, name="ident")
        make_identity(nc, ident[:])

        adj_v = adj.rearrange("(p b) j -> p b j", b=NB)
        x_v = x.rearrange("(c u p e) d -> c u p e d", c=2, u=2, e=2)
        w_v = weight.rearrange("(g t p) f -> g p t f", g=2, t=4)
        out_v = out.rearrange("(p b) f -> p b f", b=NB)

        araw, agrp, acod, asca = [], [], [], []
        for q in range(NB // 2):
            araw.append(keep.tile([P, 2 * 1024], BF16, name="araw%d" % q))
            agrp.append(keep.tile([P, 2 * 1024], BF16, name="agrp%d" % q, align_bytes=64))
            acod.append(keep.tile([P, 2 * 256], U32, name="acod%d" % q, align_bytes=64))
            asca.append(keep.tile([P, 2 * 256], U8, name="asca%d" % q, align_bytes=64))
        xraw, xgrp, xcod, xsca = {}, {}, {}, {}
        wgrp, wcod, wsca = {}, {}, {}
        axgrp, axcod, axsca = {}, {}, {}
        for h in range(2):
            for c in range(2):
                xraw[h, c] = keep.tile([P, 4, HALF], BF16, name="xraw%d%d" % (h, c))
                xgrp[h, c] = keep.tile([P, 4 * HALF], BF16, name="xgrp%d%d" % (h, c), align_bytes=64)
                xcod[h, c] = keep.tile([P, HALF], U32, name="xcod%d%d" % (h, c), align_bytes=64)
                xsca[h, c] = keep.tile([P, HALF], U8, name="xsca%d%d" % (h, c), align_bytes=64)
                wgrp[h, c] = keep.tile([P, 4 * HALF], BF16, name="wgrp%d%d" % (h, c), align_bytes=64)
                wcod[h, c] = keep.tile([P, HALF], U32, name="wcod%d%d" % (h, c), align_bytes=64)
                wsca[h, c] = keep.tile([P, HALF], U8, name="wsca%d%d" % (h, c), align_bytes=64)
            for q in range(NB // 2):
                axgrp[h, q] = keep.tile([P, 2 * HALF], BF16, name="axgrp%d%d" % (h, q), align_bytes=64)
                axcod[h, q] = keep.tile([P, 2 * P], U32, name="axcod%d%d" % (h, q), align_bytes=64)
                axsca[h, q] = keep.tile([P, 2 * P], U8, name="axsca%d%d" % (h, q), align_bytes=64)
        wraw = [keep.tile([P, 4, 1024], BF16, name="wraw%d" % g) for g in range(2)]

        def load_adj(q, blocks=(0, 1)):
            lo, n = blocks[0], len(blocks)
            nc.sync.dma_start(
                out=araw[q][:, 1024 * lo : 1024 * (lo + n)].rearrange("p (b j) -> p b j", b=n),
                in_=adj_v[:, 2 * q + lo : 2 * q + lo + n, :],
            )

        def load_x(h, c, lo=0, hi=HALF):
            for u in range(2):
                nc.sync.dma_start(
                    out=xraw[h, c][:, 2 * u : 2 * u + 2, lo:hi],
                    in_=x_v[c, u][:, :, HALF * h + lo : HALF * h + hi],
                )

        def load_w(g, lo=0, hi=1024):
            nc.sync.dma_start(out=wraw[g][:, :, lo:hi], in_=w_v[g][:, :, lo:hi])

        def transpose_adj(b, engine=None):
            q, r = b // 2, b % 2
            words = araw[q][:].bitcast(F32)
            gwords = agrp[q][:].bitcast(F32)
            tp = psum.tile([P, 4, P], F32, name="tp", tag="bank")
            for wb in range(4):
                lo = HALF * r + P * wb
                nc.tensor.transpose(tp[:, wb, :], words[:, lo : lo + P], ident[:])
            copy_on(
                engine or nc.scalar,
                gwords[:, HALF * r : HALF * (r + 1)].rearrange("p (g i u) -> p g i u", g=2, u=2),
                tp[:].rearrange("p (g u) i -> p g i u", u=2),
            )

        def keep_clock_up(tile_2d, times):
            n = min(HALF, tile_2d.shape[1])
            warm = psum.tile([P, HALF], F32, name="warm", tag="bank")
            for i in range(times):
                nc.tensor.matmul(out=warm[:, :n], lhsT=tile_2d[:, :P], rhs=tile_2d[:, :n], start=True, stop=True)

        def quantise_adj(q, blocks=(0, 1)):
            lo, hi = blocks[0], blocks[-1] + 1
            quantise(
                acod[q][:, 256 * lo : 256 * hi], asca[q][:, 256 * lo : 256 * hi], agrp[q][:, 1024 * lo : 1024 * hi]
            )

        def regroup_x(h, c, engine, lo=0, hi=HALF):
            dst, src = regroup_views(xgrp[h, c][:, 4 * lo : 4 * hi], xraw[h, c][:, :, lo:hi])
            copy_on(engine, dst, src)

        def quantise_x(h, c, lo=0, hi=HALF):
            quantise(xcod[h, c][:, lo:hi], xsca[h, c][:, lo:hi], xgrp[h, c][:, 4 * lo : 4 * hi])

        def regroup_w(fh, g, engine, lo=0, hi=HALF):
            dst, src = regroup_views(
                wgrp[g, fh][:, 4 * lo : 4 * hi], wraw[g][:, :, HALF * fh + lo : HALF * fh + hi]
            )
            copy_on(engine, dst, src)

        def quantise_w(fh, g):
            quantise(wcod[g, fh][:], wsca[g, fh][:], wgrp[g, fh][:])

        acc1 = {}

        def stage1_passes(h, b, tiles):
            q, r = b // 2, b % 2
            if (h, b) not in acc1:
                acc1[h, b] = psum.tile([P, 4, P], F32, name="acc1", tag="bank")
            for t in tiles:
                for c in range(2):
                    lo = 2 * P * r + P * c
                    nc.tensor.matmul_mx(
                        out=acc1[h, b][:, t, :],
                        lhsT=xcod[h, c][:, P * t : P * (t + 1)].bitcast(FP8X4),
                        lhsT_scale=xsca[h, c][:, P * t : P * (t + 1)],
                        rhs=acod[q][:, lo : lo + P].bitcast(FP8X4),
                        rhs_scale=asca[q][:, lo : lo + P],
                        start=(c == 0),
                        stop=(c == 1),
                    )

        def stage1_out(h, b, engine):
            q, r = b // 2, b % 2
            copy_on(
                engine,
                axgrp[h, q][:, HALF * r : HALF * (r + 1)].rearrange("p (i t) -> p i t", t=4),
                acc1[h, b][:].rearrange("p t i -> p i t"),
            )

        def stage1(h, b, engine=None):
            stage1_passes(h, b, range(4))
            stage1_out(h, b, engine or nc.scalar)

        def quantise_ax(h, q):
            quantise(axcod[h, q][:], axsca[h, q][:], axgrp[h, q][:])

        def stage2(fh, b, engines):
            q, r = b // 2, b % 2
            n = HALF // len(engines)
            for i, engine in enumerate(engines):
                acc = psum.tile([P, n], F32, name="acc2", tag="bank")
                for h in range(2):
                    nc.tensor.matmul_mx(
                        out=acc[:],
                        lhsT=axcod[h, q][:, P * r : P * (r + 1)].bitcast(FP8X4),
                        lhsT_scale=axsca[h, q][:, P * r : P * (r + 1)],
                        rhs=wcod[h, fh][:, n * i : n * (i + 1)].bitcast(FP8X4),
                        rhs_scale=wsca[h, fh][:, n * i : n * (i + 1)],
                        start=(h == 0),
                        stop=(h == 1),
                    )
                res = keep.tile([P, n], F32, name="res%d%d%d" % (fh, b, i))
                copy_on(engine, res[:], acc[:])
                lo = HALF * fh + n * i
                nc.sync.dma_start(out=out_v[:, b, lo : lo + n], in_=res[:])

        V, S = nc.vector, nc.scalar
        with tc.manual_schedule():
            load_adj(0)
            load_adj(1)
            load_x(0, 0)
            load_x(0, 1)
            load_adj(2)
            load_adj(3)
            load_x(1, 0)
            load_x(1, 1)
            for g in range(2):
                load_w(g)
            keep_clock_up(zeros[:], 6)
            transpose_adj(0)
            transpose_adj(1)
            keep_clock_up(zeros[:], 2)
            transpose_adj(2)
            transpose_adj(3)
            keep_clock_up(zeros[:], 2)
            quantise_adj(0)
            regroup_x(0, 0, V, 0, HALF - X_SCALAR_COLS)
            regroup_x(0, 0, S, HALF - X_SCALAR_COLS, HALF)
            quantise_x(0, 0)
            regroup_x(0, 1, V, 0, HALF - X_SCALAR_COLS)
            regroup_x(0, 1, S, HALF - X_SCALAR_COLS, HALF)
            quantise_adj(1)
            keep_clock_up(xraw[0, 0][:, 3, :], 2)
            keep_clock_up(xraw[0, 1][:, 3, :], 3)
            transpose_adj(4)
            transpose_adj(5)
            keep_clock_up(zeros[:], 1)
            transpose_adj(6)
            transpose_adj(7)
            keep_clock_up(zeros[:], 1)
            quantise_x(0, 1)
            quantise_adj(2)
            regroup_x(1, 0, V)
            quantise_adj(3)
            regroup_x(1, 1, V)
            quantise_x(1, 0)
            quantise_x(1, 1)
            for b in range(NB):
                stage1(0, b)

            for b in range(NB):
                stage1(1, b)
            for g in range(2):
                regroup_w(0, g, V)
                quantise_ax(0, 2 * g)
                quantise_ax(0, 2 * g + 1)
                quantise_w(0, g)
            quantise_ax(1, 0)
            quantise_ax(1, 1)
            for g in range(2):
                regroup_w(1, g, V)
                quantise_ax(1, 2 + g)
            for g in range(2):
                quantise_w(1, g)
            for b in range(NB):
                stage2(0, b, (S,))
            for b in range(NB):
                stage2(1, b, (V if b % 2 == 0 else S,))
